import numpy as np
import ml_dtypes


def mxq(x, axis, fmt="e4m3"):
    dtype, down = {"e4m3": (ml_dtypes.float8_e4m3fn, 7), "e5m2": (ml_dtypes.float8_e5m2, 14)}[fmt]
    v = np.moveaxis(np.asarray(x, np.float32).astype(ml_dtypes.bfloat16).astype(np.float64), axis, -1)
    blocks = v.reshape(v.shape[:-1] + (-1, 32))
    amax = np.abs(blocks).max(-1, keepdims=True)
    byte = np.maximum(np.where(amax > 0, np.frexp(amax)[1] - 1 + 127, 0) - down, 1)
    scale = np.exp2(byte - 127.0)
    codes = (blocks / scale).astype(np.float32).astype(dtype).astype(np.float64)
    return np.moveaxis((codes * scale).reshape(v.shape), -1, axis)


WIDE = False


def mx_kscale(k):
    if not WIDE:
        return np.ones(k)
    levels = np.array([10, -10, 5, -5, 0])
    a = np.random.permutation(np.resize(levels, k // 512 * 4)).reshape(k // 512, 4)
    idx = np.arange(k)
    return np.exp2(a[idx // 512, idx % 128 // 32])


BF16 = ml_dtypes.bfloat16


def bf(x):
    return np.asarray(x, np.float32).astype(BF16)


def f64(x):
    return np.asarray(x).astype(np.float64)


B, S, D, H, HD, F = 4, 2048, 1024, 2, 64, 4096
E = H * HD
CURV = 1.0


def lift(space):
    t = np.sqrt(np.sum(space * space, -1, keepdims=True) + 1.0 / CURV)
    return np.concatenate([t, space], -1)


def setup_inputs():
    s = mx_kscale(D)
    return {"x_space": bf(np.random.standard_normal((B, S, D)) * 2.0 / np.sqrt(D)),
            "ln1_w": bf((1.0 + 0.1 * np.random.standard_normal(D)) * s),
            "wq": bf(np.random.standard_normal((D, E)) * 0.5 / np.sqrt(D) / s[:, None]),
            "wk": bf(np.random.standard_normal((D, E)) * 0.5 / np.sqrt(D) / s[:, None]),
            "wv": bf(np.random.standard_normal((D, E)) * 0.25 / np.sqrt(D) / s[:, None])}


def reference(x_space, ln1_w, wq, wk, wv):
    s = f64(x_space)
    rms = np.sqrt(np.mean(s * s, -1, keepdims=True) + 1e-6)
    nq = mxq(s / rms * f64(ln1_w), 2, "e4m3")
    q = lift((nq @ mxq(f64(wq), 0, "e4m3")).reshape(B, S, H, HD))
    k = lift((nq @ mxq(f64(wk), 0, "e4m3")).reshape(B, S, H, HD))
    v = lift((nq @ mxq(f64(wv), 0, "e4m3")).reshape(B, S, H, HD))
    return q, k, v

@@ -1,0 +1,185 @@
+from contextlib import ExitStack
+
+import concourse.mybir as mybir
+from concourse.masks import make_identity
+
+FLOPS = 2 * 4 * 2048 * 1024 * 384
+
+F32 = mybir.dt.float32
+BF16 = mybir.dt.bfloat16
+U32 = mybir.dt.uint32
+U8 = mybir.dt.uint8
+FP8X4 = mybir.dt.float8_e4m3fn_x4
+ACT = mybir.ActivationFunctionType
+ALU = mybir.AluOpType
+
+P = 128
+PACK = 4
+K_PASS = P * PACK
+D = 1024
+PASSES = D // K_PASS
+TOKENS = 4 * 2048
+TILES = 4
+GROUP = TILES * P
+GROUPS = TOKENS // GROUP
+HEADS = 2
+HD = 64
+E = HEADS * HD
+OUTS = 3
+QK = 2 * E
+EPS = 1e-6
+
+
+def quantise_weights(nc, const, stage, wq, wk, wv):
+    raw = stage.tile([P, PASSES, PACK, OUTS * E], BF16)
+    for o, w in enumerate((wq, wk, wv)):
+        for g in range(PASSES):
+            nc.sync.dma_start(
+                out=raw[:, g, :, o * E : (o + 1) * E],
+                in_=w[g * K_PASS : (g + 1) * K_PASS, :].rearrange("(t p) n -> p t n", p=P),
+            )
+    operands = []
+    for name, first, cols in (("qk", 0, QK), ("v", QK, E)):
+        grouped = stage.tile([P, PASSES, cols, PACK], BF16, name="w_grouped_" + name, align_bytes=64)
+        for g in range(PASSES):
+            nc.vector.tensor_copy(
+                out=grouped[:, g, :, :],
+                in_=raw[:, g, :, first : first + cols].rearrange("p t c -> p c t"),
+            )
+        codes = const.tile([P, PASSES, cols], U32, name="w_codes_" + name, align_bytes=64)
+        scales = const.tile([P, PASSES, cols], U8, name="w_scales_" + name, align_bytes=64)
+        operands.append((first, cols, grouped, codes, scales))
+    for first, cols, grouped, codes, scales in operands:
+        nc.vector.quantize_mx(
+            out=codes[:].rearrange("p g c -> p (g c)").bitcast(FP8X4),
+            scales=scales[:].rearrange("p g c -> p (g c)"),
+            in_=grouped[:].rearrange("p g c t -> p (g c t)"),
+        )
+    return [(first, cols, codes, scales) for first, cols, grouped, codes, scales in operands]
+
+
+def gain_by_partition(nc, const, stage, psum, ident, ln1_w):
+    rows = stage.tile([P, P], BF16)
+    nc.vector.memset(rows[:], 0.0)
+    nc.sync.dma_start(out=rows[0 : D // P, :], in_=ln1_w.rearrange("(j p) -> j p", p=P))
+    rows_f32 = stage.tile([P, P], F32)
+    nc.vector.tensor_copy(out=rows_f32[:], in_=rows[:])
+    turned = psum.tile([P, PACK, P], F32, name="turned")
+    nc.tensor.transpose(turned[:, 0, :], rows_f32[:], ident[:])
+    gain = const.tile([P, PASSES, PACK], F32)
+    nc.vector.tensor_copy(
+        out=gain[:].rearrange("p g t -> p (g t)"), in_=turned[:, 0, 0 : D // P]
+    )
+    return gain
+
+
+def tile_ltransformerdecoderblock_pa_t_kernel(
+    tc, x_space, ln1_w, wq, wk, wv, out_0, out_1, out_2
+):
+    nc = tc.nc
+    x_rows = x_space.rearrange("b s d -> (b s) d")
+    out_rows = [o.rearrange("b s h c -> (b s) (h c)") for o in (out_0, out_1, out_2)]
+
+    with ExitStack() as ctx:
+        const = ctx.enter_context(tc.tile_pool(name="const", bufs=1))
+        stage = ctx.enter_context(tc.tile_pool(name="stage", bufs=1))
+        x_pool = ctx.enter_context(tc.tile_pool(name="x", bufs=4))
+        sq_pool = ctx.enter_context(tc.tile_pool(name="sq", bufs=2))
+        y_pool = ctx.enter_context(tc.tile_pool(name="y", bufs=3))
+        n_pool = ctx.enter_context(tc.tile_pool(name="n", bufs=2))
+        o_pool = ctx.enter_context(tc.tile_pool(name="o", bufs=3))
+        small = ctx.enter_context(tc.tile_pool(name="small", bufs=4))
+        psum_t = ctx.enter_context(tc.psum_pool(name="psum_t", bufs=4))
+        psum_o = ctx.enter_context(tc.psum_pool(name="psum_o", bufs=4))
+
+        def load_group(i):
+            x_sb = x_pool.tile([P, TILES, D], BF16, name="x_sb")
+            nc.sync.dma_start(
+                out=x_sb[:],
+                in_=x_rows[i * GROUP : (i + 1) * GROUP, :].rearrange("(p j) d -> p j d", j=TILES),
+            )
+            return x_sb
+
+        x_tiles = [load_group(0)]
+
+        ident = const.tile([P, P], F32)
+        make_identity(nc, ident[:])
+        gain = gain_by_partition(nc, const, stage, psum_t, ident, ln1_w)
+        weights = quantise_weights(nc, const, stage, wq, wk, wv)
+
+        for i in range(GROUPS):
+            x_sb = x_tiles[i]
+            if i + 1 < GROUPS:
+                x_tiles.append(load_group(i + 1))
+
+            squares = sq_pool.tile([P, TILES, D], BF16, name="squares")
+            sum_sq = small.tile([P, TILES], F32, name="sum_sq")
+            for j in range(TILES):
+                nc.scalar.activation(
+                    out=squares[:, j, :], in_=x_sb[:, j, :], func=ACT.Square,
+                    accum_out=sum_sq[:, j : j + 1],
+                )
+            rms = small.tile([P, TILES], F32, name="rms")
+            nc.scalar.activation(out=rms[:], in_=sum_sq[:], func=ACT.Sqrt, scale=1.0 / D, bias=EPS)
+            rstd = small.tile([P, TILES], F32, name="rstd")
+            nc.vector.reciprocal(out=rstd[:], in_=rms[:])
+
+            y = y_pool.tile([P, TILES, D], F32, name="y")
+            for j in range(TILES):
+                nc.gpsimd.tensor_scalar(
+                    out=y[:, j, :], in0=x_sb[:, j, :], scalar1=rstd[:, j : j + 1], scalar2=1.0,
+                    op0=ALU.mult, op1=ALU.mult,
+                )
+
+            n_grouped = n_pool.tile([P, TILES, PASSES, P, PACK], BF16, name="n_grouped", align_bytes=64)
+            for j in range(TILES):
+                for g in range(PASSES):
+                    turned = psum_t.tile([P, PACK, P], F32, name="turned")
+                    for t in range(PACK):
+                        k0 = g * K_PASS + t * P
+                        nc.tensor.transpose(turned[:, t, :], y[:, j, k0 : k0 + P], ident[:])
+                    nc.vector.tensor_tensor(
+                        out=n_grouped[:, j, g, :, :],
+                        in0=turned[:].rearrange("p t r -> p r t"),
+                        in1=gain[:, g, :].unsqueeze(1).to_broadcast([P, P, PACK]),
+                        op=ALU.mult,
+                    )
+            n_codes = n_pool.tile([P, TILES, PASSES, P], U32, name="n_codes", align_bytes=64)
+            n_scales = n_pool.tile([P, TILES, PASSES, P], U8, name="n_scales", align_bytes=64)
+            nc.vector.quantize_mx(
+                out=n_codes[:].rearrange("p j g r -> p (j g r)").bitcast(FP8X4),
+                scales=n_scales[:].rearrange("p j g r -> p (j g r)"),
+                in_=n_grouped[:].rearrange("p j g r t -> p (j g r t)"),
+            )
+
+            lifted = o_pool.tile([P, OUTS, TILES, HEADS, 1 + HD], F32, name="lifted")
+            head_sq = small.tile([P, OUTS, TILES, HEADS], F32, name="head_sq")
+            for j in range(TILES):
+                product = psum_o.tile([P, OUTS * E], F32, name="product")
+                for first, cols, w_codes, w_scales in weights:
+                    for g in range(PASSES):
+                        nc.tensor.matmul_mx(
+                            out=product[:, first : first + cols],
+                            lhsT=n_codes[:, j, g, :].bitcast(FP8X4),
+                            lhsT_scale=n_scales[:, j, g, :],
+                            rhs=w_codes[:, g, :].bitcast(FP8X4),
+                            rhs_scale=w_scales[:, g, :],
+                            start=(g == 0),
+                            stop=(g == PASSES - 1),
+                        )
+                by_head = product[:].rearrange("p (o h c) -> p o h c", o=OUTS, h=HEADS)
+                nc.scalar.copy(out=lifted[:, :, j, :, 1:], in_=by_head)
+                squared = o_pool.tile([P, OUTS, HEADS, HD], F32, name="squared")
+                nc.scalar.activation(out=squared[:], in_=by_head, func=ACT.Square)
+                nc.vector.tensor_reduce(
+                    out=head_sq[:, :, j, :], in_=squared[:], axis=mybir.AxisListType.X, op=ALU.add
+                )
+            nc.scalar.activation(out=lifted[:, :, :, :, 0], in_=head_sq[:], func=ACT.Sqrt, bias=1.0)
+
+            for o in range(OUTS):
+                nc.sync.dma_start(
+                    out=out_rows[o][i * GROUP : (i + 1) * GROUP, :].rearrange(
+                        "(p j) c -> p (j c)", j=TILES
+                    ),
+                    in_=lifted[:, o, :, :, :].rearrange("p j h c -> p (j h c)"),
+                )

@@ -22,12 +22,23 @@ TOKENS = 4 * 2048
 TILES = 4
 GROUP = TILES * P
 GROUPS = TOKENS // GROUP
+UNITS = GROUPS * TILES
 HEADS = 2
 HD = 64
 E = HEADS * HD
 OUTS = 3
 QK = 2 * E
 EPS = 1e-6
+
+SUM_LEAD = 8
+SCALE_LEAD = 3
+TURN_LEAD = 1
+QUANT_LAG = 1
+PROJECT_LAG = 2
+LIFT_LAG = 3
+HEAD_SUM_LAG = 4
+STORE_LAG = 5
+LOAD_AHEAD = 2
 
 
 def quantise_weights(nc, const, stage, wq, wk, wv):
@@ -83,103 +94,162 @@ def tile_ltransformerdecoderblock_pa_t_kernel(
     with ExitStack() as ctx:
         const = ctx.enter_context(tc.tile_pool(name="const", bufs=1))
         stage = ctx.enter_context(tc.tile_pool(name="stage", bufs=1))
-        x_pool = ctx.enter_context(tc.tile_pool(name="x", bufs=4))
-        sq_pool = ctx.enter_context(tc.tile_pool(name="sq", bufs=2))
-        y_pool = ctx.enter_context(tc.tile_pool(name="y", bufs=3))
-        n_pool = ctx.enter_context(tc.tile_pool(name="n", bufs=2))
-        o_pool = ctx.enter_context(tc.tile_pool(name="o", bufs=3))
-        small = ctx.enter_context(tc.tile_pool(name="small", bufs=4))
+        x_pool = ctx.enter_context(tc.tile_pool(name="x", bufs=LOAD_AHEAD + 3))
+        by_group = ctx.enter_context(tc.tile_pool(name="by_group", bufs=4))
+        by_unit = ctx.enter_context(tc.tile_pool(name="by_unit", bufs=4))
         psum_t = ctx.enter_context(tc.psum_pool(name="psum_t", bufs=4))
         psum_o = ctx.enter_context(tc.psum_pool(name="psum_o", bufs=4))
+        ctx.enter_context(tc.manual_schedule())
+
+        x_sb = {}
+        sum_sq = {}
+        rms = {}
+        rstd = {}
+        lifted = {}
+        head_sq = {}
+        y = {}
+        turned = {}
+        n_grouped = {}
+        n_codes = {}
+        n_scales = {}
+        product = {}
+        squared = {}
 
         def load_group(i):
-            x_sb = x_pool.tile([P, TILES, D], BF16, name="x_sb")
+            x_sb[i] = x_pool.tile([P, TILES, D], BF16, name="x_sb")
             nc.sync.dma_start(
-                out=x_sb[:],
+                out=x_sb[i][:],
                 in_=x_rows[i * GROUP : (i + 1) * GROUP, :].rearrange("(p j) d -> p j d", j=TILES),
             )
-            return x_sb
 
-        x_tiles = [load_group(0)]
-
-        ident = const.tile([P, P], F32)
-        make_identity(nc, ident[:])
-        gain = gain_by_partition(nc, const, stage, psum_t, ident, ln1_w)
-        weights = quantise_weights(nc, const, stage, wq, wk, wv)
-
-        for i in range(GROUPS):
-            x_sb = x_tiles[i]
-            if i + 1 < GROUPS:
-                x_tiles.append(load_group(i + 1))
-
-            squares = sq_pool.tile([P, TILES, D], BF16, name="squares")
-            sum_sq = small.tile([P, TILES], F32, name="sum_sq")
-            for j in range(TILES):
+        def sum_squares(u):
+            i, j = divmod(u, TILES)
+            if j == 0:
+                sum_sq[i] = by_group.tile([P, TILES], F32, name="sum_sq")
+            scratch = by_unit.tile([P, D], BF16, name="scratch")
+            nc.scalar.activation(
+                out=scratch[:], in_=x_sb[i][:, j, :], func=ACT.Square,
+                accum_out=sum_sq[i][:, j : j + 1],
+            )
+            if j == TILES - 1:
+                rms[i] = by_group.tile([P, TILES], F32, name="rms")
                 nc.scalar.activation(
-                    out=squares[:, j, :], in_=x_sb[:, j, :], func=ACT.Square,
-                    accum_out=sum_sq[:, j : j + 1],
-                )
-            rms = small.tile([P, TILES], F32, name="rms")
-            nc.scalar.activation(out=rms[:], in_=sum_sq[:], func=ACT.Sqrt, scale=1.0 / D, bias=EPS)
-            rstd = small.tile([P, TILES], F32, name="rstd")
-            nc.vector.reciprocal(out=rstd[:], in_=rms[:])
-
-            y = y_pool.tile([P, TILES, D], F32, name="y")
-            for j in range(TILES):
-                nc.gpsimd.tensor_scalar(
-                    out=y[:, j, :], in0=x_sb[:, j, :], scalar1=rstd[:, j : j + 1], scalar2=1.0,
-                    op0=ALU.mult, op1=ALU.mult,
+                    out=rms[i][:], in_=sum_sq[i][:], func=ACT.Sqrt, scale=1.0 / D, bias=EPS
                 )
 
-            n_grouped = n_pool.tile([P, TILES, PASSES, P, PACK], BF16, name="n_grouped", align_bytes=64)
-            for j in range(TILES):
-                for g in range(PASSES):
-                    turned = psum_t.tile([P, PACK, P], F32, name="turned")
-                    for t in range(PACK):
-                        k0 = g * K_PASS + t * P
-                        nc.tensor.transpose(turned[:, t, :], y[:, j, k0 : k0 + P], ident[:])
-                    nc.vector.tensor_tensor(
-                        out=n_grouped[:, j, g, :, :],
-                        in0=turned[:].rearrange("p t r -> p r t"),
-                        in1=gain[:, g, :].unsqueeze(1).to_broadcast([P, P, PACK]),
-                        op=ALU.mult,
-                    )
-            n_codes = n_pool.tile([P, TILES, PASSES, P], U32, name="n_codes", align_bytes=64)
-            n_scales = n_pool.tile([P, TILES, PASSES, P], U8, name="n_scales", align_bytes=64)
-            nc.vector.quantize_mx(
-                out=n_codes[:].rearrange("p j g r -> p (j g r)").bitcast(FP8X4),
-                scales=n_scales[:].rearrange("p j g r -> p (j g r)"),
-                in_=n_grouped[:].rearrange("p j g r t -> p (j g r t)"),
+        def invert_rms(i):
+            rstd[i] = by_group.tile([P, TILES], F32, name="rstd")
+            nc.vector.reciprocal(out=rstd[i][:], in_=rms[i][:])
+
+        def scale_rows(u):
+            i, j = divmod(u, TILES)
+            y[u] = by_unit.tile([P, D], F32, name="y")
+            nc.gpsimd.tensor_scalar(
+                out=y[u][:], in0=x_sb[i][:, j, :], scalar1=rstd[i][:, j : j + 1], scalar2=1.0,
+                op0=ALU.mult, op1=ALU.mult,
             )
 
-            lifted = o_pool.tile([P, OUTS, TILES, HEADS, 1 + HD], F32, name="lifted")
-            head_sq = small.tile([P, OUTS, TILES, HEADS], F32, name="head_sq")
-            for j in range(TILES):
-                product = psum_o.tile([P, OUTS * E], F32, name="product")
-                for first, cols, w_codes, w_scales in weights:
-                    for g in range(PASSES):
-                        nc.tensor.matmul_mx(
-                            out=product[:, first : first + cols],
-                            lhsT=n_codes[:, j, g, :].bitcast(FP8X4),
-                            lhsT_scale=n_scales[:, j, g, :],
-                            rhs=w_codes[:, g, :].bitcast(FP8X4),
-                            rhs_scale=w_scales[:, g, :],
-                            start=(g == 0),
-                            stop=(g == PASSES - 1),
-                        )
-                by_head = product[:].rearrange("p (o h c) -> p o h c", o=OUTS, h=HEADS)
-                nc.scalar.copy(out=lifted[:, :, j, :, 1:], in_=by_head)
-                squared = o_pool.tile([P, OUTS, HEADS, HD], F32, name="squared")
-                nc.scalar.activation(out=squared[:], in_=by_head, func=ACT.Square)
-                nc.vector.tensor_reduce(
-                    out=head_sq[:, :, j, :], in_=squared[:], axis=mybir.AxisListType.X, op=ALU.add
-                )
-            nc.scalar.activation(out=lifted[:, :, :, :, 0], in_=head_sq[:], func=ACT.Sqrt, bias=1.0)
+        def turn(u):
+            for g in range(PASSES):
+                turned[u, g] = psum_t.tile([P, PACK, P], F32, name="turned")
+                for t in range(PACK):
+                    k0 = g * K_PASS + t * P
+                    nc.tensor.transpose(turned[u, g][:, t, :], y[u][:, k0 : k0 + P], ident[:])
 
+        def apply_gain(u):
+            n_grouped[u] = by_unit.tile([P, PASSES, P, PACK], BF16, name="n_grouped", align_bytes=64)
+            for g in range(PASSES):
+                nc.vector.tensor_tensor(
+                    out=n_grouped[u][:, g, :, :],
+                    in0=turned[u, g][:].rearrange("p t r -> p r t"),
+                    in1=gain[:, g, :].unsqueeze(1).to_broadcast([P, P, PACK]),
+                    op=ALU.mult,
+                )
+
+        def quantise(u):
+            n_codes[u] = by_unit.tile([P, PASSES, P], U32, name="n_codes", align_bytes=64)
+            n_scales[u] = by_unit.tile([P, PASSES, P], U8, name="n_scales", align_bytes=64)
+            nc.vector.quantize_mx(
+                out=n_codes[u][:].rearrange("p g r -> p (g r)").bitcast(FP8X4),
+                scales=n_scales[u][:].rearrange("p g r -> p (g r)"),
+                in_=n_grouped[u][:].rearrange("p g r t -> p (g r t)"),
+            )
+
+        def project(u):
+            product[u] = psum_o.tile([P, OUTS * E], F32, name="product")
+            for first, cols, w_codes, w_scales in weights:
+                for g in range(PASSES):
+                    nc.tensor.matmul_mx(
+                        out=product[u][:, first : first + cols],
+                        lhsT=n_codes[u][:, g, :].bitcast(FP8X4),
+                        lhsT_scale=n_scales[u][:, g, :],
+                        rhs=w_codes[:, g, :].bitcast(FP8X4),
+                        rhs_scale=w_scales[:, g, :],
+                        start=(g == 0),
+                        stop=(g == PASSES - 1),
+                    )
+
+        def lift(u):
+            i, j = divmod(u, TILES)
+            if j == 0:
+                lifted[i] = by_group.tile([P, OUTS, TILES, HEADS, 1 + HD], F32, name="lifted")
+            by_head = product[u][:].rearrange("p (o h c) -> p o h c", o=OUTS, h=HEADS)
+            nc.scalar.copy(out=lifted[i][:, :, j, :, 1:], in_=by_head)
+            squared[u] = by_unit.tile([P, OUTS, HEADS, HD], F32, name="squared")
+            nc.scalar.activation(out=squared[u][:], in_=by_head, func=ACT.Square)
+
+        def sum_heads(u):
+            i, j = divmod(u, TILES)
+            if j == 0:
+                head_sq[i] = by_group.tile([P, OUTS, TILES, HEADS], F32, name="head_sq")
+            nc.vector.tensor_reduce(
+                out=head_sq[i][:, :, j, :], in_=squared[u][:], axis=mybir.AxisListType.X, op=ALU.add
+            )
+
+        def store_group(i):
+            nc.scalar.activation(
+                out=lifted[i][:, :, :, :, 0], in_=head_sq[i][:], func=ACT.Sqrt, bias=1.0
+            )
             for o in range(OUTS):
                 nc.sync.dma_start(
                     out=out_rows[o][i * GROUP : (i + 1) * GROUP, :].rearrange(
                         "(p j) c -> p (j c)", j=TILES
                     ),
-                    in_=lifted[:, o, :, :, :].rearrange("p j h c -> p (j h c)"),
+                    in_=lifted[i][:, o, :, :, :].rearrange("p j h c -> p (j h c)"),
                 )
+
+        load_group(0)
+        ident = const.tile([P, P], F32)
+        make_identity(nc, ident[:])
+        gain = gain_by_partition(nc, const, stage, psum_t, ident, ln1_w)
+        weights = quantise_weights(nc, const, stage, wq, wk, wv)
+        for i in range(1, LOAD_AHEAD):
+            load_group(i)
+
+        def is_unit(u):
+            return 0 <= u < UNITS
+
+        for s in range(-SUM_LEAD, UNITS + STORE_LAG):
+            if is_unit(s + SUM_LEAD) and (s + SUM_LEAD) % TILES == 0:
+                if (s + SUM_LEAD) // TILES + LOAD_AHEAD < GROUPS:
+                    load_group((s + SUM_LEAD) // TILES + LOAD_AHEAD)
+            if is_unit(s - STORE_LAG) and (s - STORE_LAG) % TILES == TILES - 1:
+                store_group((s - STORE_LAG) // TILES)
+            if is_unit(s + SUM_LEAD):
+                sum_squares(s + SUM_LEAD)
+            if is_unit(s + SCALE_LEAD + 1) and (s + SCALE_LEAD + 1) % TILES == 0:
+                invert_rms((s + SCALE_LEAD + 1) // TILES)
+            if is_unit(s + SCALE_LEAD):
+                scale_rows(s + SCALE_LEAD)
+            if is_unit(s - PROJECT_LAG):
+                project(s - PROJECT_LAG)
+            if is_unit(s + TURN_LEAD):
+                turn(s + TURN_LEAD)
+            if is_unit(s):
+                apply_gain(s)
+            if is_unit(s - QUANT_LAG):
+                quantise(s - QUANT_LAG)
+            if is_unit(s - LIFT_LAG):
+                lift(s - LIFT_LAG)
+            if is_unit(s - HEAD_SUM_LAG):
+                sum_heads(s - HEAD_SUM_LAG)

@@ -27,7 +27,7 @@ HEADS = 2
 HD = 64
 E = HEADS * HD
 OUTS = 3
-QK = 2 * E
+MOVING = 512
 EPS = 1e-6
 
 SUM_LEAD = 8
@@ -42,31 +42,26 @@ LOAD_AHEAD = 2
 
 
 def quantise_weights(nc, const, stage, wq, wk, wv):
-    raw = stage.tile([P, PASSES, PACK, OUTS * E], BF16)
-    for o, w in enumerate((wq, wk, wv)):
+    raw = stage.tile([P, PASSES, PACK, MOVING], BF16)
+    for o, w in enumerate((wq, wk, wv, wv)):
         for g in range(PASSES):
             nc.sync.dma_start(
                 out=raw[:, g, :, o * E : (o + 1) * E],
                 in_=w[g * K_PASS : (g + 1) * K_PASS, :].rearrange("(t p) n -> p t n", p=P),
             )
-    operands = []
-    for name, first, cols in (("qk", 0, QK), ("v", QK, E)):
-        grouped = stage.tile([P, PASSES, cols, PACK], BF16, name="w_grouped_" + name, align_bytes=64)
-        for g in range(PASSES):
-            nc.vector.tensor_copy(
-                out=grouped[:, g, :, :],
-                in_=raw[:, g, :, first : first + cols].rearrange("p t c -> p c t"),
-            )
-        codes = const.tile([P, PASSES, cols], U32, name="w_codes_" + name, align_bytes=64)
-        scales = const.tile([P, PASSES, cols], U8, name="w_scales_" + name, align_bytes=64)
-        operands.append((first, cols, grouped, codes, scales))
-    for first, cols, grouped, codes, scales in operands:
-        nc.vector.quantize_mx(
-            out=codes[:].rearrange("p g c -> p (g c)").bitcast(FP8X4),
-            scales=scales[:].rearrange("p g c -> p (g c)"),
-            in_=grouped[:].rearrange("p g c t -> p (g c t)"),
+    grouped = stage.tile([P, PASSES, MOVING, PACK], BF16, align_bytes=64)
+    for g in range(PASSES):
+        nc.vector.tensor_copy(
+            out=grouped[:, g, :, :], in_=raw[:, g, :, :].rearrange("p t c -> p c t")
         )
-    return [(first, cols, codes, scales) for first, cols, grouped, codes, scales in operands]
+    w_codes = const.tile([P, PASSES, MOVING], U32, align_bytes=64)
+    w_scales = const.tile([P, PASSES, MOVING], U8, align_bytes=64)
+    nc.vector.quantize_mx(
+        out=w_codes[:].rearrange("p g c -> p (g c)").bitcast(FP8X4),
+        scales=w_scales[:].rearrange("p g c -> p (g c)"),
+        in_=grouped[:].rearrange("p g c t -> p (g c t)"),
+    )
+    return w_codes, w_scales
 
 
 def gain_by_partition(nc, const, stage, psum, ident, ln1_w):
@@ -176,24 +171,23 @@ def tile_ltransformerdecoderblock_pa_t_kernel(
             )
 
         def project(u):
-            product[u] = psum_o.tile([P, OUTS * E], F32, name="product")
-            for first, cols, w_codes, w_scales in weights:
-                for g in range(PASSES):
-                    nc.tensor.matmul_mx(
-                        out=product[u][:, first : first + cols],
-                        lhsT=n_codes[u][:, g, :].bitcast(FP8X4),
-                        lhsT_scale=n_scales[u][:, g, :],
-                        rhs=w_codes[:, g, :].bitcast(FP8X4),
-                        rhs_scale=w_scales[:, g, :],
-                        start=(g == 0),
-                        stop=(g == PASSES - 1),
-                    )
+            product[u] = psum_o.tile([P, MOVING], F32, name="product")
+            for g in range(PASSES):
+                nc.tensor.matmul_mx(
+                    out=product[u][:],
+                    lhsT=n_codes[u][:, g, :].bitcast(FP8X4),
+                    lhsT_scale=n_scales[u][:, g, :],
+                    rhs=w_codes[:, g, :].bitcast(FP8X4),
+                    rhs_scale=w_scales[:, g, :],
+                    start=(g == 0),
+                    stop=(g == PASSES - 1),
+                )
 
         def lift(u):
             i, j = divmod(u, TILES)
             if j == 0:
                 lifted[i] = by_group.tile([P, OUTS, TILES, HEADS, 1 + HD], F32, name="lifted")
-            by_head = product[u][:].rearrange("p (o h c) -> p o h c", o=OUTS, h=HEADS)
+            by_head = product[u][:, 0 : OUTS * E].rearrange("p (o h c) -> p o h c", o=OUTS, h=HEADS)
             nc.scalar.copy(out=lifted[i][:, :, j, :, 1:], in_=by_head)
             squared[u] = by_unit.tile([P, OUTS, HEADS, HD], F32, name="squared")
             nc.scalar.activation(out=squared[u][:], in_=by_head, func=ACT.Square)
@@ -222,7 +216,7 @@ def tile_ltransformerdecoderblock_pa_t_kernel(
         ident = const.tile([P, P], F32)
         make_identity(nc, ident[:])
         gain = gain_by_partition(nc, const, stage, psum_t, ident, ln1_w)
-        weights = quantise_weights(nc, const, stage, wq, wk, wv)
+        w_codes, w_scales = quantise_weights(nc, const, stage, wq, wk, wv)
         for i in range(1, LOAD_AHEAD):
             load_group(i)
 

@@ -27,41 +27,46 @@ HEADS = 2
 HD = 64
 E = HEADS * HD
 OUTS = 3
-MOVING = 512
+QK = 2 * E
 EPS = 1e-6
 
+LOAD_LEAD = 16
 SUM_LEAD = 8
-SCALE_LEAD = 3
+SCALE_LEAD = 2
 TURN_LEAD = 1
 QUANT_LAG = 1
 PROJECT_LAG = 2
 LIFT_LAG = 3
-HEAD_SUM_LAG = 4
-STORE_LAG = 5
-LOAD_AHEAD = 2
+HEAD_SUM_LAG = 6
+STORE_LAG = HEAD_SUM_LAG + 1
 
 
 def quantise_weights(nc, const, stage, wq, wk, wv):
-    raw = stage.tile([P, PASSES, PACK, MOVING], BF16)
-    for o, w in enumerate((wq, wk, wv, wv)):
+    raw = stage.tile([P, PASSES, PACK, OUTS * E], BF16)
+    for o, w in enumerate((wq, wk, wv)):
         for g in range(PASSES):
             nc.sync.dma_start(
                 out=raw[:, g, :, o * E : (o + 1) * E],
                 in_=w[g * K_PASS : (g + 1) * K_PASS, :].rearrange("(t p) n -> p t n", p=P),
             )
-    grouped = stage.tile([P, PASSES, MOVING, PACK], BF16, align_bytes=64)
-    for g in range(PASSES):
-        nc.vector.tensor_copy(
-            out=grouped[:, g, :, :], in_=raw[:, g, :, :].rearrange("p t c -> p c t")
+    operands = []
+    for name, first, cols in (("qk", 0, QK), ("v", QK, E)):
+        grouped = stage.tile([P, PASSES, cols, PACK], BF16, name="w_grouped_" + name, align_bytes=64)
+        for g in range(PASSES):
+            nc.vector.tensor_copy(
+                out=grouped[:, g, :, :],
+                in_=raw[:, g, :, first : first + cols].rearrange("p t c -> p c t"),
+            )
+        codes = const.tile([P, PASSES, cols], U32, name="w_codes_" + name, align_bytes=64)
+        scales = const.tile([P, PASSES, cols], U8, name="w_scales_" + name, align_bytes=64)
+        operands.append((first, cols, grouped, codes, scales))
+    for first, cols, grouped, codes, scales in operands:
+        nc.vector.quantize_mx(
+            out=codes[:].rearrange("p g c -> p (g c)").bitcast(FP8X4),
+            scales=scales[:].rearrange("p g c -> p (g c)"),
+            in_=grouped[:].rearrange("p g c t -> p (g c t)"),
         )
-    w_codes = const.tile([P, PASSES, MOVING], U32, align_bytes=64)
-    w_scales = const.tile([P, PASSES, MOVING], U8, align_bytes=64)
-    nc.vector.quantize_mx(
-        out=w_codes[:].rearrange("p g c -> p (g c)").bitcast(FP8X4),
-        scales=w_scales[:].rearrange("p g c -> p (g c)"),
-        in_=grouped[:].rearrange("p g c t -> p (g c t)"),
-    )
-    return w_codes, w_scales
+    return [(first, cols, codes, scales) for first, cols, grouped, codes, scales in operands]
 
 
 def gain_by_partition(nc, const, stage, psum, ident, ln1_w):
@@ -89,9 +94,10 @@ def tile_ltransformerdecoderblock_pa_t_kernel(
     with ExitStack() as ctx:
         const = ctx.enter_context(tc.tile_pool(name="const", bufs=1))
         stage = ctx.enter_context(tc.tile_pool(name="stage", bufs=1))
-        x_pool = ctx.enter_context(tc.tile_pool(name="x", bufs=LOAD_AHEAD + 3))
+        x_pool = ctx.enter_context(tc.tile_pool(name="x", bufs=(LOAD_LEAD - SCALE_LEAD) // TILES + 2))
         by_group = ctx.enter_context(tc.tile_pool(name="by_group", bufs=4))
         by_unit = ctx.enter_context(tc.tile_pool(name="by_unit", bufs=4))
+        squares = ctx.enter_context(tc.tile_pool(name="squares", bufs=HEAD_SUM_LAG - LIFT_LAG + 2))
         psum_t = ctx.enter_context(tc.psum_pool(name="psum_t", bufs=4))
         psum_o = ctx.enter_context(tc.psum_pool(name="psum_o", bufs=4))
         ctx.enter_context(tc.manual_schedule())
@@ -110,12 +116,12 @@ def tile_ltransformerdecoderblock_pa_t_kernel(
         product = {}
         squared = {}
 
-        def load_group(i):
-            x_sb[i] = x_pool.tile([P, TILES, D], BF16, name="x_sb")
-            nc.sync.dma_start(
-                out=x_sb[i][:],
-                in_=x_rows[i * GROUP : (i + 1) * GROUP, :].rearrange("(p j) d -> p j d", j=TILES),
-            )
+        def load_unit(u):
+            i, j = divmod(u, TILES)
+            if j == 0:
+                x_sb[i] = x_pool.tile([P, TILES, D], BF16, name="x_sb")
+            group_rows = x_rows[i * GROUP : (i + 1) * GROUP, :].rearrange("(p j) d -> p j d", j=TILES)
+            nc.sync.dma_start(out=x_sb[i][:, j, :], in_=group_rows[:, j, :])
 
         def sum_squares(u):
             i, j = divmod(u, TILES)
@@ -171,25 +177,26 @@ def tile_ltransformerdecoderblock_pa_t_kernel(
             )
 
         def project(u):
-            product[u] = psum_o.tile([P, MOVING], F32, name="product")
-            for g in range(PASSES):
-                nc.tensor.matmul_mx(
-                    out=product[u][:],
-                    lhsT=n_codes[u][:, g, :].bitcast(FP8X4),
-                    lhsT_scale=n_scales[u][:, g, :],
-                    rhs=w_codes[:, g, :].bitcast(FP8X4),
-                    rhs_scale=w_scales[:, g, :],
-                    start=(g == 0),
-                    stop=(g == PASSES - 1),
-                )
+            product[u] = psum_o.tile([P, OUTS * E], F32, name="product")
+            for first, cols, w_codes, w_scales in weights:
+                for g in range(PASSES):
+                    nc.tensor.matmul_mx(
+                        out=product[u][:, first : first + cols],
+                        lhsT=n_codes[u][:, g, :].bitcast(FP8X4),
+                        lhsT_scale=n_scales[u][:, g, :],
+                        rhs=w_codes[:, g, :].bitcast(FP8X4),
+                        rhs_scale=w_scales[:, g, :],
+                        start=(g == 0),
+                        stop=(g == PASSES - 1),
+                    )
 
         def lift(u):
             i, j = divmod(u, TILES)
             if j == 0:
                 lifted[i] = by_group.tile([P, OUTS, TILES, HEADS, 1 + HD], F32, name="lifted")
-            by_head = product[u][:, 0 : OUTS * E].rearrange("p (o h c) -> p o h c", o=OUTS, h=HEADS)
+            by_head = product[u][:].rearrange("p (o h c) -> p o h c", o=OUTS, h=HEADS)
             nc.scalar.copy(out=lifted[i][:, :, j, :, 1:], in_=by_head)
-            squared[u] = by_unit.tile([P, OUTS, HEADS, HD], F32, name="squared")
+            squared[u] = squares.tile([P, OUTS, HEADS, HD], F32, name="squared")
             nc.scalar.activation(out=squared[u][:], in_=by_head, func=ACT.Square)
 
         def sum_heads(u):
@@ -212,27 +219,25 @@ def tile_ltransformerdecoderblock_pa_t_kernel(
                     in_=lifted[i][:, o, :, :, :].rearrange("p j h c -> p (j h c)"),
                 )
 
-        load_group(0)
+        for u in range(TILES):
+            load_unit(u)
         ident = const.tile([P, P], F32)
         make_identity(nc, ident[:])
         gain = gain_by_partition(nc, const, stage, psum_t, ident, ln1_w)
-        w_codes, w_scales = quantise_weights(nc, const, stage, wq, wk, wv)
-        for i in range(1, LOAD_AHEAD):
-            load_group(i)
+        for u in range(TILES, LOAD_LEAD - SUM_LEAD):
+            load_unit(u)
+        weights = quantise_weights(nc, const, stage, wq, wk, wv)
 
         def is_unit(u):
             return 0 <= u < UNITS
 
         for s in range(-SUM_LEAD, UNITS + STORE_LAG):
-            if is_unit(s + SUM_LEAD) and (s + SUM_LEAD) % TILES == 0:
-                if (s + SUM_LEAD) // TILES + LOAD_AHEAD < GROUPS:
-                    load_group((s + SUM_LEAD) // TILES + LOAD_AHEAD)
+            if is_unit(s + LOAD_LEAD):
+                load_unit(s + LOAD_LEAD)
             if is_unit(s - STORE_LAG) and (s - STORE_LAG) % TILES == TILES - 1:
                 store_group((s - STORE_LAG) // TILES)
             if is_unit(s + SUM_LEAD):
                 sum_squares(s + SUM_LEAD)
-            if is_unit(s + SCALE_LEAD + 1) and (s + SCALE_LEAD + 1) % TILES == 0:
-                invert_rms((s + SCALE_LEAD + 1) // TILES)
             if is_unit(s + SCALE_LEAD):
                 scale_rows(s + SCALE_LEAD)
             if is_unit(s - PROJECT_LAG):
@@ -247,3 +252,5 @@ def tile_ltransformerdecoderblock_pa_t_kernel(
                 lift(s - LIFT_LAG)
             if is_unit(s - HEAD_SUM_LAG):
                 sum_heads(s - HEAD_SUM_LAG)
+            if is_unit(s + SCALE_LEAD + 1) and (s + SCALE_LEAD + 1) % TILES == 0:
+                invert_rms((s + SCALE_LEAD + 1) // TILES)

from contextlib import ExitStack

import concourse.mybir as mybir
from concourse.masks import make_identity

FLOPS = 2 * 4 * 2048 * 1024 * 384

F32 = mybir.dt.float32
BF16 = mybir.dt.bfloat16
U32 = mybir.dt.uint32
U8 = mybir.dt.uint8
FP8X4 = mybir.dt.float8_e4m3fn_x4
ACT = mybir.ActivationFunctionType
ALU = mybir.AluOpType

P = 128
PACK = 4
K_PASS = P * PACK
D = 1024
PASSES = D // K_PASS
TOKENS = 4 * 2048
TILES = 4
GROUP = TILES * P
GROUPS = TOKENS // GROUP
UNITS = GROUPS * TILES
HEADS = 2
HD = 64
E = HEADS * HD
OUTS = 3
QK = 2 * E
EPS = 1e-6

LOAD_LEAD = 16
SUM_LEAD = 8
SCALE_LEAD = 2
TURN_LEAD = 1
QUANT_LAG = 1
PROJECT_LAG = 2
LIFT_LAG = 3
HEAD_SUM_LAG = 6
STORE_LAG = HEAD_SUM_LAG + 1


def quantise_weights(nc, const, stage, wq, wk, wv):
    raw = stage.tile([P, PASSES, PACK, OUTS * E], BF16)
    for o, w in enumerate((wq, wk, wv)):
        for g in range(PASSES):
            nc.sync.dma_start(
                out=raw[:, g, :, o * E : (o + 1) * E],
                in_=w[g * K_PASS : (g + 1) * K_PASS, :].rearrange("(t p) n -> p t n", p=P),
            )
    operands = []
    for name, first, cols in (("qk", 0, QK), ("v", QK, E)):
        grouped = stage.tile([P, PASSES, cols, PACK], BF16, name="w_grouped_" + name, align_bytes=64)
        for g in range(PASSES):
            nc.vector.tensor_copy(
                out=grouped[:, g, :, :],
                in_=raw[:, g, :, first : first + cols].rearrange("p t c -> p c t"),
            )
        codes = const.tile([P, PASSES, cols], U32, name="w_codes_" + name, align_bytes=64)
        scales = const.tile([P, PASSES, cols], U8, name="w_scales_" + name, align_bytes=64)
        operands.append((first, cols, grouped, codes, scales))
    for first, cols, grouped, codes, scales in operands:
        nc.vector.quantize_mx(
            out=codes[:].rearrange("p g c -> p (g c)").bitcast(FP8X4),
            scales=scales[:].rearrange("p g c -> p (g c)"),
            in_=grouped[:].rearrange("p g c t -> p (g c t)"),
        )
    return [(first, cols, codes, scales) for first, cols, grouped, codes, scales in operands]


def gain_by_partition(nc, const, stage, psum, ident, ln1_w):
    rows = stage.tile([P, P], BF16)
    nc.vector.memset(rows[:], 0.0)
    nc.sync.dma_start(out=rows[0 : D // P, :], in_=ln1_w.rearrange("(j p) -> j p", p=P))
    rows_f32 = stage.tile([P, P], F32)
    nc.vector.tensor_copy(out=rows_f32[:], in_=rows[:])
    turned = psum.tile([P, PACK, P], F32, name="turned")
    nc.tensor.transpose(turned[:, 0, :], rows_f32[:], ident[:])
    gain = const.tile([P, PASSES, PACK], F32)
    nc.vector.tensor_copy(
        out=gain[:].rearrange("p g t -> p (g t)"), in_=turned[:, 0, 0 : D // P]
    )
    return gain


def tile_ltransformerdecoderblock_pa_t_kernel(
    tc, x_space, ln1_w, wq, wk, wv, out_0, out_1, out_2
):
    nc = tc.nc
    x_rows = x_space.rearrange("b s d -> (b s) d")
    out_rows = [o.rearrange("b s h c -> (b s) (h c)") for o in (out_0, out_1, out_2)]

    with ExitStack() as ctx:
        const = ctx.enter_context(tc.tile_pool(name="const", bufs=1))
        stage = ctx.enter_context(tc.tile_pool(name="stage", bufs=1))
        x_pool = ctx.enter_context(tc.tile_pool(name="x", bufs=(LOAD_LEAD - SCALE_LEAD) // TILES + 2))
        by_group = ctx.enter_context(tc.tile_pool(name="by_group", bufs=4))
        by_unit = ctx.enter_context(tc.tile_pool(name="by_unit", bufs=4))
        squares = ctx.enter_context(tc.tile_pool(name="squares", bufs=HEAD_SUM_LAG - LIFT_LAG + 2))
        psum_t = ctx.enter_context(tc.psum_pool(name="psum_t", bufs=4))
        psum_o = ctx.enter_context(tc.psum_pool(name="psum_o", bufs=4))
        ctx.enter_context(tc.manual_schedule())

        x_sb = {}
        sum_sq = {}
        rms = {}
        rstd = {}
        lifted = {}
        head_sq = {}
        y = {}
        turned = {}
        n_grouped = {}
        n_codes = {}
        n_scales = {}
        product = {}
        squared = {}

        def load_unit(u):
            i, j = divmod(u, TILES)
            if j == 0:
                x_sb[i] = x_pool.tile([P, TILES, D], BF16, name="x_sb")
            group_rows = x_rows[i * GROUP : (i + 1) * GROUP, :].rearrange("(p j) d -> p j d", j=TILES)
            nc.sync.dma_start(out=x_sb[i][:, j, :], in_=group_rows[:, j, :])

        def sum_squares(u):
            i, j = divmod(u, TILES)
            if j == 0:
                sum_sq[i] = by_group.tile([P, TILES], F32, name="sum_sq")
            scratch = by_unit.tile([P, D], BF16, name="scratch")
            nc.scalar.activation(
                out=scratch[:], in_=x_sb[i][:, j, :], func=ACT.Square,
                accum_out=sum_sq[i][:, j : j + 1],
            )
            if j == TILES - 1:
                rms[i] = by_group.tile([P, TILES], F32, name="rms")
                nc.scalar.activation(
                    out=rms[i][:], in_=sum_sq[i][:], func=ACT.Sqrt, scale=1.0 / D, bias=EPS
                )

        def invert_rms(i):
            rstd[i] = by_group.tile([P, TILES], F32, name="rstd")
            nc.vector.reciprocal(out=rstd[i][:], in_=rms[i][:])

        def scale_rows(u):
            i, j = divmod(u, TILES)
            y[u] = by_unit.tile([P, D], F32, name="y")
            nc.gpsimd.tensor_scalar(
                out=y[u][:], in0=x_sb[i][:, j, :], scalar1=rstd[i][:, j : j + 1], scalar2=1.0,
                op0=ALU.mult, op1=ALU.mult,
            )

        def turn(u):
            for g in range(PASSES):
                turned[u, g] = psum_t.tile([P, PACK, P], F32, name="turned")
                for t in range(PACK):
                    k0 = g * K_PASS + t * P
                    nc.tensor.transpose(turned[u, g][:, t, :], y[u][:, k0 : k0 + P], ident[:])

        def apply_gain(u):
            n_grouped[u] = by_unit.tile([P, PASSES, P, PACK], BF16, name="n_grouped", align_bytes=64)
            for g in range(PASSES):
                nc.vector.tensor_tensor(
                    out=n_grouped[u][:, g, :, :],
                    in0=turned[u, g][:].rearrange("p t r -> p r t"),
                    in1=gain[:, g, :].unsqueeze(1).to_broadcast([P, P, PACK]),
                    op=ALU.mult,
                )

        def quantise(u):
            n_codes[u] = by_unit.tile([P, PASSES, P], U32, name="n_codes", align_bytes=64)
            n_scales[u] = by_unit.tile([P, PASSES, P], U8, name="n_scales", align_bytes=64)
            nc.vector.quantize_mx(
                out=n_codes[u][:].rearrange("p g r -> p (g r)").bitcast(FP8X4),
                scales=n_scales[u][:].rearrange("p g r -> p (g r)"),
                in_=n_grouped[u][:].rearrange("p g r t -> p (g r t)"),
            )

        def project(u):
            product[u] = psum_o.tile([P, OUTS * E], F32, name="product")
            for first, cols, w_codes, w_scales in weights:
                for g in range(PASSES):
                    nc.tensor.matmul_mx(
                        out=product[u][:, first : first + cols],
                        lhsT=n_codes[u][:, g, :].bitcast(FP8X4),
                        lhsT_scale=n_scales[u][:, g, :],
                        rhs=w_codes[:, g, :].bitcast(FP8X4),
                        rhs_scale=w_scales[:, g, :],
                        start=(g == 0),
                        stop=(g == PASSES - 1),
                    )

        def lift(u):
            i, j = divmod(u, TILES)
            if j == 0:
                lifted[i] = by_group.tile([P, OUTS, TILES, HEADS, 1 + HD], F32, name="lifted")
            by_head = product[u][:].rearrange("p (o h c) -> p o h c", o=OUTS, h=HEADS)
            nc.scalar.copy(out=lifted[i][:, :, j, :, 1:], in_=by_head)
            squared[u] = squares.tile([P, OUTS, HEADS, HD], F32, name="squared")
            nc.scalar.activation(out=squared[u][:], in_=by_head, func=ACT.Square)

        def sum_heads(u):
            i, j = divmod(u, TILES)
            if j == 0:
                head_sq[i] = by_group.tile([P, OUTS, TILES, HEADS], F32, name="head_sq")
            nc.vector.tensor_reduce(
                out=head_sq[i][:, :, j, :], in_=squared[u][:], axis=mybir.AxisListType.X, op=ALU.add
            )

        def store_group(i):
            nc.scalar.activation(
                out=lifted[i][:, :, :, :, 0], in_=head_sq[i][:], func=ACT.Sqrt, bias=1.0
            )
            for o in range(OUTS):
                nc.sync.dma_start(
                    out=out_rows[o][i * GROUP : (i + 1) * GROUP, :].rearrange(
                        "(p j) c -> p (j c)", j=TILES
                    ),
                    in_=lifted[i][:, o, :, :, :].rearrange("p j h c -> p (j h c)"),
                )

        for u in range(TILES):
            load_unit(u)
        ident = const.tile([P, P], F32)
        make_identity(nc, ident[:])
        gain = gain_by_partition(nc, const, stage, psum_t, ident, ln1_w)
        for u in range(TILES, LOAD_LEAD - SUM_LEAD):
            load_unit(u)
        weights = quantise_weights(nc, const, stage, wq, wk, wv)

        def is_unit(u):
            return 0 <= u < UNITS

        for s in range(-SUM_LEAD, UNITS + STORE_LAG):
            if is_unit(s + LOAD_LEAD):
                load_unit(s + LOAD_LEAD)
            if is_unit(s - STORE_LAG) and (s - STORE_LAG) % TILES == TILES - 1:
                store_group((s - STORE_LAG) // TILES)
            if is_unit(s + SUM_LEAD):
                sum_squares(s + SUM_LEAD)
            if is_unit(s + SCALE_LEAD):
                scale_rows(s + SCALE_LEAD)
            if is_unit(s - PROJECT_LAG):
                project(s - PROJECT_LAG)
            if is_unit(s + TURN_LEAD):
                turn(s + TURN_LEAD)
            if is_unit(s):
                apply_gain(s)
            if is_unit(s - QUANT_LAG):
                quantise(s - QUANT_LAG)
            if is_unit(s - LIFT_LAG):
                lift(s - LIFT_LAG)
            if is_unit(s - HEAD_SUM_LAG):
                sum_heads(s - HEAD_SUM_LAG)
            if is_unit(s + SCALE_LEAD + 1) and (s + SCALE_LEAD + 1) % TILES == 0:
                invert_rms((s + SCALE_LEAD + 1) // TILES)
